import numpy as np
import ml_dtypes


def mxq(x, axis, fmt="e4m3"):
    dtype, down = {"e4m3": (ml_dtypes.float8_e4m3fn, 7), "e5m2": (ml_dtypes.float8_e5m2, 14)}[fmt]
    v = np.moveaxis(np.asarray(x, np.float32).astype(ml_dtypes.bfloat16).astype(np.float64), axis, -1)
    blocks = v.reshape(v.shape[:-1] + (-1, 32))
    amax = np.abs(blocks).max(-1, keepdims=True)
    byte = np.maximum(np.where(amax > 0, np.frexp(amax)[1] - 1 + 127, 0) - down, 1)
    scale = np.exp2(byte - 127.0)
    codes = (blocks / scale).astype(np.float32).astype(dtype).astype(np.float64)
    return np.moveaxis((codes * scale).reshape(v.shape), -1, axis)


WIDE = False


def mx_kscale(k):
    if not WIDE:
        return np.ones(k)
    levels = np.array([18, -18])
    if k % 512:
        return np.exp2(np.random.permutation(np.resize(levels, k // 32))).repeat(32)
    a = np.empty((k // 512, 16))
    for p in range(k // 512):
        a[p, :8] = np.random.permutation(np.resize(levels, 8))
        for g in range(8):
            far = levels[np.abs(levels - a[p, g]) >= 10]
            a[p, g + 8] = far[np.random.randint(len(far))]
    return np.exp2(a.ravel()).repeat(32)


BF16 = ml_dtypes.bfloat16


def bf(x):
    return np.asarray(x, np.float32).astype(BF16)


def f64(x):
    return np.asarray(x).astype(np.float64)


B, D, K = 1536, 512, 4


def setup_inputs():
    a = np.maximum(mx_kscale(B), 1.0)[:, None, None]
    u = mx_kscale(D)[None, :, None]
    x0 = bf(np.random.standard_normal((B, D, K)))
    mu = bf(np.random.standard_normal((D, K)) * 0.3)
    w0 = bf(np.eye(D)[None] + np.random.standard_normal((K, D, D)) * 0.7 / np.sqrt(D))
    g = bf(np.random.standard_normal((B, D, K)) * np.exp2(np.random.randint(-6, 1, (B, 1, 1))) / a * u)
    return {"x": bf(f64(x0) * a), "mu_track": mu, "Std_inv_track": bf(f64(w0) / u), "grad_out": g}


def reference(x, mu_track, Std_inv_track, grad_out):
    g = f64(grad_out)
    w = f64(Std_inv_track)
    x_cnt = f64(x) - f64(mu_track)[None]
    gd = mxq(g, 1, "e5m2").transpose(2, 0, 1)
    wd = mxq(w, 1, "e4m3")
    dx = (gd @ wd).transpose(1, 2, 0)
    gb = mxq(g, 0, "e5m2").transpose(2, 1, 0)
    xb = mxq(x_cnt, 0, "e4m3").transpose(2, 0, 1)
    dw = gb @ xb
    return dx, dw

@@ -1,0 +1,258 @@
+from contextlib import ExitStack
+
+import concourse.mybir as mybir
+from concourse.masks import make_identity
+
+B, D, K = 1536, 512, 4
+FLOPS = 2 * 2 * B * D * D * K
+
+F32 = mybir.dt.float32
+BF16 = mybir.dt.bfloat16
+U32 = mybir.dt.uint32
+U8 = mybir.dt.uint8
+E4M3 = mybir.dt.float8_e4m3fn_x4
+E5M2 = mybir.dt.float8_e5m2_x4
+ALU = mybir.AluOpType
+
+P = 128
+J = 4
+G = B // (P * J)
+DK = D * K
+N = G * J
+
+TRICK = []
+VA = [1,5,9]
+GI = []
+SLOT = [0,0,1,2,3,4,5,5,6,7,8,8]
+
+
+def tile_clusternorm1dv3_v_kernel(tc, x, mu, w, g, dx, dw):
+    nc = tc.nc
+    xv = x.rearrange("(g p j) d k -> g p j (d k)", p=P, j=J)
+    gv = g.rearrange("(g p j) d k -> g p j (d k)", p=P, j=J)
+    dxv = dx.rearrange("(g p j) d k -> g p j (d k)", p=P, j=J)
+    muv = mu.rearrange("(o d) k -> o (d k)", o=1)
+
+    with ExitStack() as ctx:
+        keep = ctx.enter_context(tc.tile_pool(name="keep", bufs=1))
+        raw = ctx.enter_context(tc.tile_pool(name="raw", bufs=2))
+        stage = ctx.enter_context(tc.tile_pool(name="stage", bufs=2))
+        pmu = ctx.enter_context(tc.psum_pool(name="pmu", bufs=1))
+        ptr = ctx.enter_context(tc.psum_pool(name="ptr", bufs=2))
+        pac = ctx.enter_context(tc.psum_pool(name="pac", bufs=4))
+
+        ident = keep.tile([P, P], F32)
+        make_identity(nc, ident[:])
+
+        gq = keep.tile([P, G, 4, K, P], U32, align_bytes=64)
+        gs = keep.tile([P, G, 4, K, P], U8, align_bytes=64)
+        xq = keep.tile([P, G, K, D], U32, align_bytes=64)
+        xs = keep.tile([P, G, K, D], U8, align_bytes=64)
+        wq = keep.tile([P, K, D], U32, align_bytes=64)
+        ws = keep.tile([P, K, D], U8, align_bytes=64)
+
+        mu0 = keep.tile([P, DK], BF16)
+        nc.gpsimd.memset(mu0[:], 0.0)
+        ones = keep.tile([P, P], BF16)
+        nc.gpsimd.memset(ones[:], 1.0)
+        mups = pmu.tile([P, DK], BF16)
+
+        g_raw, x_raw, w_raw = {}, {}, {}
+        gd, gdq, gds, ps, m, o, ga, xa = {}, {}, {}, {}, {}, {}, {}, {}
+
+        def load_w(k):
+            if k % 2 == 0:
+                t = stage.tile([P, 2, J, D], BF16, name="wraw", tag="o", bufs=3)
+                w_raw[k // 2] = t
+            nc.sync.dma_start(out=w_raw[k // 2][:, k % 2], in_=w[k].rearrange("(p j) e -> p j e", j=J))
+
+        def load_g(i, j):
+            if i not in g_raw:
+                t = raw.tile([P, J, DK], BF16, name="graw", bufs=2)
+                g_raw[i] = t
+            nc.sync.dma_start(out=g_raw[i][:, j, :], in_=gv[i, :, j, :])
+
+        def load_x(i, h):
+            if i not in x_raw:
+                t = raw.tile([P, J, DK], BF16, name="xraw", bufs=2)
+                x_raw[i] = t
+            nc.sync.dma_start(out=x_raw[i][:, :, h * 1024:(h + 1) * 1024], in_=xv[i, :, :, h * 1024:(h + 1) * 1024])
+
+        wa = {}
+
+        def wcopy(k, eng):
+            t = stage.tile([P, D, J], BF16, align_bytes=64, name="wa", bufs=2)
+            wa[k] = t
+            eng(out=t[:], in_=w_raw[k // 2][:, k % 2].rearrange("p j e -> p e j"))
+
+        def wquant(k):
+            nc.vector.quantize_mx(out=wq[:, k, :].bitcast(E4M3), scales=ws[:, k, :], in_=wa[k][:].rearrange("p e j -> p (e j)"))
+
+        def mu_spread():
+            for c in range(4):
+                nc.tensor.matmul(mups[:, c * 512:(c + 1) * 512], lhsT=ones[:], rhs=mu0[:, c * 512:(c + 1) * 512], start=True, stop=True)
+
+        tr = {}
+
+        def T(n):
+            i, j = divmod(n, J)
+            gw = g_raw[i][:].bitcast(F32)
+            for kk in range(2):
+                if True:
+                    t_ = ptr.tile([P, J, P], F32, name="tr")
+                    tr[n, kk] = t_
+                    for t in range(J):
+                        nc.tensor.transpose(t_[:, t, :], gw[:, j, 2 * t + kk:1024:8], ident[:])
+
+        def C(n):
+            gd_t = stage.tile([P, K, P, J], BF16, align_bytes=64, name="gd", bufs=2)
+            gd[n] = gd_t
+            for kk in range(2):
+                if True:
+                    nc.scalar.copy(out=gd_t[:, 2 * kk:2 * kk + 2], in_=tr[n, kk][:].bitcast(BF16).rearrange("q t (m e) -> q e m t", e=2))
+
+        def Q(n):
+            q = stage.tile([P, K, P], U32, align_bytes=64, name="gdq")
+            s = stage.tile([P, K, P], U8, align_bytes=64, name="gds")
+            gdq[n], gds[n] = q, s
+            nc.vector.quantize_mx(out=q[:].rearrange("p k m -> p (k m)").bitcast(E5M2),
+                                  scales=s[:].rearrange("p k m -> p (k m)"),
+                                  in_=gd[n][:].rearrange("p k m t -> p (k m t)"))
+
+        def M(n):
+            for k in range(K):
+                a = pac.tile([P, D], F32, name="acc")
+                ps[n, k] = a
+                nc.tensor.matmul_mx(out=a[:], lhsT=gdq[n][:, k, :].bitcast(E5M2), lhsT_scale=gds[n][:, k, :],
+                                    rhs=wq[:, k, :].bitcast(E4M3), rhs_scale=ws[:, k, :], start=True, stop=True)
+
+        def E(n):
+            m_t = stage.tile([P, K, D], F32, name="m", bufs=2)
+            m[n] = m_t
+            for k in range(K):
+                nc.scalar.copy(out=m_t[:, k, :], in_=ps[n, k][:])
+
+        def I(n):
+            i, j = divmod(n, J)
+            o_t = stage.tile([P, D, K], F32, name="o", tag="o", bufs=3)
+            if n in GI:
+                nc.gpsimd.tensor_scalar(out=o_t[:], in0=m[n][:].rearrange("p k e -> p e k"), scalar1=1.0, scalar2=0.0, op0=ALU.mult, op1=ALU.add)
+            else:
+                nc.vector.tensor_copy(out=o_t[:], in_=m[n][:].rearrange("p k e -> p e k"))
+            nc.sync.dma_start(out=dxv[i, :, j, :], in_=o_t[:].rearrange("p e k -> p (e k)"))
+
+        def A(u):
+            i, c = divmod(u, 4)
+            t = stage.tile([P, K, P, J], BF16, align_bytes=64, name="ga", bufs=3)
+            ga[u] = t
+            eng = nc.vector.tensor_copy if u in VA else nc.scalar.copy
+            eng(out=t[:].rearrange("p k d j -> p d k j"),
+                in_=g_raw[i][:, :, c * 512:(c + 1) * 512].rearrange("p j (d k) -> p d k j", k=K))
+
+        def QG(u):
+            i, c = divmod(u, 4)
+            nc.vector.quantize_mx(out=gq[:, i, c].rearrange("p k d -> p (k d)").bitcast(E5M2),
+                                  scales=gs[:, i, c].rearrange("p k d -> p (k d)"),
+                                  in_=ga[u][:].rearrange("p k d j -> p (k d j)"))
+
+        def X(u):
+            i, c = divmod(u, 4)
+            h = u // 2
+            if u % 2 == 0:
+                t = stage.tile([P, K, 2 * P, J], BF16, align_bytes=64, name="xa", bufs=2)
+                xa[h] = t
+            b = (c % 2) * P
+            nc.vector.tensor_sub(out=xa[h][:, :, b:b + P, :].rearrange("p k e j -> p e k j"),
+                                 in0=x_raw[i][:, :, c * 512:(c + 1) * 512].rearrange("p j (e k) -> p e k j", k=K),
+                                 in1=mups[:, c * 512:(c + 1) * 512].rearrange("p (e k) -> p e k", k=K).unsqueeze(3).to_broadcast([P, P, K, J]))
+
+        def QX(h):
+            i, b = divmod(h, 2)
+            for k in range(K):
+                nc.vector.quantize_mx(out=xq[:, i, k, b * 256:(b + 1) * 256].bitcast(E4M3), scales=xs[:, i, k, b * 256:(b + 1) * 256],
+                                      in_=xa[h][:, k].rearrange("p e j -> p (e j)"))
+
+        def Dw(k):
+            for c in range(4):
+                a = pac.tile([P, D], F32, name="acc")
+                ps["w", k, c] = a
+                for i in range(G):
+                    nc.tensor.matmul_mx(out=a[:], lhsT=gq[:, i, c, k, :].bitcast(E5M2), lhsT_scale=gs[:, i, c, k, :],
+                                        rhs=xq[:, i, k, :].bitcast(E4M3), rhs_scale=xs[:, i, k, :],
+                                        start=(i == 0), stop=(i == G - 1))
+
+        def Fw(k, engs):
+            o_t = stage.tile([P, 4, D], F32, name="o", tag="o", bufs=3)
+            for c in range(4):
+                engs[c](out=o_t[:, c, :], in_=ps["w", k, c][:])
+            nc.sync.dma_start(out=dw[k].rearrange("(c p) e -> p c e", c=4), in_=o_t[:])
+
+        V = nc.vector.tensor_copy
+        S = nc.scalar.copy
+
+        with tc.manual_schedule():
+            load_w(0)
+            load_g(0, 0)
+            load_w(1)
+            nc.sync.dma_start(out=mu0[0:1, :], in_=muv)
+            load_x(0, 0)
+            load_w(2)
+            load_w(3)
+            load_g(0, 1)
+            load_g(0, 2)
+            load_g(0, 3)
+            load_x(0, 1)
+            for j in range(J):
+                load_g(1, j)
+            for h in range(2):
+                load_x(1, h)
+
+            T(0)
+            mu_spread()
+            wcopy(0, V)
+            C(0)
+            wcopy(1, V)
+            wquant(0)
+            Q(0)
+            wquant(1)
+            wcopy(2, S)
+            wcopy(3, V)
+            wquant(2)
+            wquant(3)
+            pend = []
+            for s in range(N):
+                toks = [u for u in range(N) if SLOT[u] == s]
+                if s + 1 < N:
+                    T(s + 1)
+                M(s)
+                if s + 1 < N:
+                    C(s + 1)
+                for u in toks:
+                    X(u)
+                    if u in VA:
+                        A(u)
+                if s > 0:
+                    I(s - 1)
+                for f in pend:
+                    f()
+                pend = []
+                E(s)
+                for u in toks:
+                    if u not in VA:
+                        A(u)
+                    pend.append(lambda u=u: QG(u))
+                    if u % 2 == 1:
+                        pend.append(lambda u=u: QX(u // 2))
+                if s + 1 < N:
+                    Q(s + 1)
+                if 3 in [u for u in toks]:
+                    for j in range(J):
+                        load_g(2, j)
+                    for h in range(2):
+                        load_x(2, h)
+                if s >= 9:
+                    Dw(s - 9)
+                    Fw(s - 9, [V, V, V, V])
+            I(N - 1)
+            Dw(3)
+            Fw(3, [S, V, S, V])

@@ -20,10 +20,16 @@ G = B // (P * J)
 DK = D * K
 N = G * J
 
-TRICK = []
-VA = [1,5,9]
-GI = []
-SLOT = [0,0,1,2,3,4,5,5,6,7,8,8]
+TOKS = [2,2,0,1,2,0,1,1,2,0,1,0]
+AE = "VVVVVVVVVSVV"
+IS = [0,5]
+FE = "VSVSVVSSVSSVSSSS"
+XE = "VPVPVPVVVVPV"
+WE = "VVSV"
+DS = [8,9,10,11]
+FL = 0
+L1 = ["w0","g00","mu","w1","w2","w3","g01","x00","x01","g02","g03","x10","x11","g10","g11","g12","g13"]
+L2 = ["x20","x21","g20","g21","g22","g23"]
 
 
 def tile_clusternorm1dv3_v_kernel(tc, x, mu, w, g, dx, dw):
@@ -37,79 +43,91 @@ def tile_clusternorm1dv3_v_kernel(tc, x, mu, w, g, dx, dw):
         keep = ctx.enter_context(tc.tile_pool(name="keep", bufs=1))
         raw = ctx.enter_context(tc.tile_pool(name="raw", bufs=2))
         stage = ctx.enter_context(tc.tile_pool(name="stage", bufs=2))
-        pmu = ctx.enter_context(tc.psum_pool(name="pmu", bufs=1))
         ptr = ctx.enter_context(tc.psum_pool(name="ptr", bufs=2))
-        pac = ctx.enter_context(tc.psum_pool(name="pac", bufs=4))
+        pac = ctx.enter_context(tc.psum_pool(name="pac", bufs=6))
 
         ident = keep.tile([P, P], F32)
         make_identity(nc, ident[:])
-
-        gq = keep.tile([P, G, 4, K, P], U32, align_bytes=64)
-        gs = keep.tile([P, G, 4, K, P], U8, align_bytes=64)
+        identb = keep.tile([P, P], BF16)
+        make_identity(nc, identb[:])
+        gq = keep.tile([P, G, K, D], U32, align_bytes=64)
+        gs = keep.tile([P, G, K, D], U8, align_bytes=64)
         xq = keep.tile([P, G, K, D], U32, align_bytes=64)
         xs = keep.tile([P, G, K, D], U8, align_bytes=64)
         wq = keep.tile([P, K, D], U32, align_bytes=64)
         ws = keep.tile([P, K, D], U8, align_bytes=64)
-
         mu0 = keep.tile([P, DK], BF16)
-        nc.gpsimd.memset(mu0[:], 0.0)
+        nc.vector.memset(mu0[:], 0.0)
         ones = keep.tile([P, P], BF16)
         nc.gpsimd.memset(ones[:], 1.0)
-        mups = pmu.tile([P, DK], BF16)
+        nones = keep.tile([P, P], BF16)
+        nc.gpsimd.memset(nones[:], -1.0)
+        mub = keep.tile([P, DK], BF16)
 
         g_raw, x_raw, w_raw = {}, {}, {}
-        gd, gdq, gds, ps, m, o, ga, xa = {}, {}, {}, {}, {}, {}, {}, {}
+        gd, gdq, gds, ps, m, ga, xa, wa, tr = {}, {}, {}, {}, {}, {}, {}, {}, {}
 
-        def load_w(k):
-            if k % 2 == 0:
-                t = stage.tile([P, 2, J, D], BF16, name="wraw", tag="o", bufs=3)
-                w_raw[k // 2] = t
-            nc.sync.dma_start(out=w_raw[k // 2][:, k % 2], in_=w[k].rearrange("(p j) e -> p j e", j=J))
+        def copier(e):
+            if e == "V":
+                return nc.vector.tensor_copy
+            if e == "S":
+                return nc.scalar.copy
 
-        def load_g(i, j):
-            if i not in g_raw:
-                t = raw.tile([P, J, DK], BF16, name="graw", bufs=2)
-                g_raw[i] = t
-            nc.sync.dma_start(out=g_raw[i][:, j, :], in_=gv[i, :, j, :])
+            def gcopy(out, in_):
+                nc.gpsimd.tensor_scalar(out=out, in0=in_, scalar1=1.0, scalar2=0.0, op0=ALU.mult, op1=ALU.add)
+            return gcopy
 
-        def load_x(i, h):
-            if i not in x_raw:
-                t = raw.tile([P, J, DK], BF16, name="xraw", bufs=2)
-                x_raw[i] = t
-            nc.sync.dma_start(out=x_raw[i][:, :, h * 1024:(h + 1) * 1024], in_=xv[i, :, :, h * 1024:(h + 1) * 1024])
+        def load(s):
+            if s == "mu":
+                nc.sync.dma_start(out=mu0[0:1, :], in_=muv)
+                return
+            i = int(s[1])
+            if s[0] == "w":
+                if i % 2 == 0:
+                    t = stage.tile([P, 2, J, D], BF16, name="wraw", tag="o", bufs=3)
+                    w_raw[i // 2] = t
+                nc.sync.dma_start(out=w_raw[i // 2][:, i % 2], in_=w[i].rearrange("(p j) e -> p j e", j=J))
+            elif s[0] == "g":
+                j = int(s[2])
+                if i not in g_raw:
+                    t = raw.tile([P, J, DK], BF16, name="graw", bufs=2)
+                    g_raw[i] = t
+                nc.sync.dma_start(out=g_raw[i][:, j, :], in_=gv[i, :, j, :])
+            else:
+                h = int(s[2])
+                if i not in x_raw:
+                    t = raw.tile([P, J, DK], BF16, name="xraw", bufs=2)
+                    x_raw[i] = t
+                nc.sync.dma_start(out=x_raw[i][:, :, h * 1024:(h + 1) * 1024], in_=xv[i, :, :, h * 1024:(h + 1) * 1024])
 
-        wa = {}
-
-        def wcopy(k, eng):
+        def wcopy(k):
             t = stage.tile([P, D, J], BF16, align_bytes=64, name="wa", bufs=2)
             wa[k] = t
-            eng(out=t[:], in_=w_raw[k // 2][:, k % 2].rearrange("p j e -> p e j"))
+            copier(WE[k])(out=t[:], in_=w_raw[k // 2][:, k % 2].rearrange("p j e -> p e j"))
 
         def wquant(k):
             nc.vector.quantize_mx(out=wq[:, k, :].bitcast(E4M3), scales=ws[:, k, :], in_=wa[k][:].rearrange("p e j -> p (e j)"))
 
         def mu_spread():
             for c in range(4):
-                nc.tensor.matmul(mups[:, c * 512:(c + 1) * 512], lhsT=ones[:], rhs=mu0[:, c * 512:(c + 1) * 512], start=True, stop=True)
-
-        tr = {}
+                t = pac.tile([P, D], F32, name="acc")
+                nc.tensor.matmul(t[:], lhsT=ones[:], rhs=mu0[:, c * 512:(c + 1) * 512], start=True, stop=True)
+                nc.scalar.copy(out=mub[:, c * 512:(c + 1) * 512], in_=t[:])
 
         def T(n):
             i, j = divmod(n, J)
             gw = g_raw[i][:].bitcast(F32)
             for kk in range(2):
-                if True:
-                    t_ = ptr.tile([P, J, P], F32, name="tr")
-                    tr[n, kk] = t_
-                    for t in range(J):
-                        nc.tensor.transpose(t_[:, t, :], gw[:, j, 2 * t + kk:1024:8], ident[:])
+                t_ = ptr.tile([P, J, P], F32, name="tr")
+                tr[n, kk] = t_
+                for t in range(J):
+                    nc.tensor.transpose(t_[:, t, :], gw[:, j, 2 * t + kk:1024:8], ident[:])
 
         def C(n):
             gd_t = stage.tile([P, K, P, J], BF16, align_bytes=64, name="gd", bufs=2)
             gd[n] = gd_t
             for kk in range(2):
-                if True:
-                    nc.scalar.copy(out=gd_t[:, 2 * kk:2 * kk + 2], in_=tr[n, kk][:].bitcast(BF16).rearrange("q t (m e) -> q e m t", e=2))
+                nc.scalar.copy(out=gd_t[:, 2 * kk:2 * kk + 2], in_=tr[n, kk][:].bitcast(BF16).rearrange("q t (m e) -> q e m t", e=2))
 
         def Q(n):
             q = stage.tile([P, K, P], U32, align_bytes=64, name="gdq")
@@ -126,133 +144,138 @@ def tile_clusternorm1dv3_v_kernel(tc, x, mu, w, g, dx, dw):
                 nc.tensor.matmul_mx(out=a[:], lhsT=gdq[n][:, k, :].bitcast(E5M2), lhsT_scale=gds[n][:, k, :],
                                     rhs=wq[:, k, :].bitcast(E4M3), rhs_scale=ws[:, k, :], start=True, stop=True)
 
-        def E(n):
-            m_t = stage.tile([P, K, D], F32, name="m", bufs=2)
-            m[n] = m_t
-            for k in range(K):
-                nc.scalar.copy(out=m_t[:, k, :], in_=ps[n, k][:])
+        def E(n, ks, e):
+            if n not in m:
+                m_t = stage.tile([P, K, D], F32, name="m", bufs=2)
+                m[n] = m_t
+            for k in ks:
+                copier(e)(out=m[n][:, k, :], in_=ps[n, k][:])
 
         def I(n):
             i, j = divmod(n, J)
             o_t = stage.tile([P, D, K], F32, name="o", tag="o", bufs=3)
-            if n in GI:
-                nc.gpsimd.tensor_scalar(out=o_t[:], in0=m[n][:].rearrange("p k e -> p e k"), scalar1=1.0, scalar2=0.0, op0=ALU.mult, op1=ALU.add)
-            else:
-                nc.vector.tensor_copy(out=o_t[:], in_=m[n][:].rearrange("p k e -> p e k"))
+            copier("S" if n in IS else "V")(out=o_t[:], in_=m[n][:].rearrange("p k e -> p e k"))
             nc.sync.dma_start(out=dxv[i, :, j, :], in_=o_t[:].rearrange("p e k -> p (e k)"))
 
         def A(u):
-            i, c = divmod(u, 4)
-            t = stage.tile([P, K, P, J], BF16, align_bytes=64, name="ga", bufs=3)
+            i, k = divmod(u, K)
+            t = stage.tile([P, D, J], BF16, align_bytes=64, name="ga", bufs=3)
             ga[u] = t
-            eng = nc.vector.tensor_copy if u in VA else nc.scalar.copy
-            eng(out=t[:].rearrange("p k d j -> p d k j"),
-                in_=g_raw[i][:, :, c * 512:(c + 1) * 512].rearrange("p j (d k) -> p d k j", k=K))
+            copier(AE[u])(out=t[:], in_=g_raw[i][:].rearrange("p j (d k) -> p d k j", k=K)[:, :, k, :])
 
         def QG(u):
-            i, c = divmod(u, 4)
-            nc.vector.quantize_mx(out=gq[:, i, c].rearrange("p k d -> p (k d)").bitcast(E5M2),
-                                  scales=gs[:, i, c].rearrange("p k d -> p (k d)"),
-                                  in_=ga[u][:].rearrange("p k d j -> p (k d j)"))
+            i, k = divmod(u, K)
+            nc.vector.quantize_mx(out=gq[:, i, k, :].bitcast(E5M2), scales=gs[:, i, k, :],
+                                  in_=ga[u][:].rearrange("p d j -> p (d j)"))
+
+        def xtile(u):
+            t = stage.tile([P, D, J], BF16, align_bytes=64, name="xa", bufs=3)
+            xa[u] = t
 
         def X(u):
-            i, c = divmod(u, 4)
-            h = u // 2
-            if u % 2 == 0:
-                t = stage.tile([P, K, 2 * P, J], BF16, align_bytes=64, name="xa", bufs=2)
-                xa[h] = t
-            b = (c % 2) * P
-            nc.vector.tensor_sub(out=xa[h][:, :, b:b + P, :].rearrange("p k e j -> p e k j"),
-                                 in0=x_raw[i][:, :, c * 512:(c + 1) * 512].rearrange("p j (e k) -> p e k j", k=K),
-                                 in1=mups[:, c * 512:(c + 1) * 512].rearrange("p (e k) -> p e k", k=K).unsqueeze(3).to_broadcast([P, P, K, J]))
+            i, k = divmod(u, K)
+            xtile(u)
+            nc.vector.tensor_sub(out=xa[u][:], in0=x_raw[i][:].rearrange("p j (e k) -> p e k j", k=K)[:, :, k, :],
+                                 in1=mub[:].rearrange("p (e k) -> p e k", k=K)[:, :, k].unsqueeze(2).to_broadcast([P, D, J]))
 
-        def QX(h):
-            i, b = divmod(h, 2)
-            for k in range(K):
-                nc.vector.quantize_mx(out=xq[:, i, k, b * 256:(b + 1) * 256].bitcast(E4M3), scales=xs[:, i, k, b * 256:(b + 1) * 256],
-                                      in_=xa[h][:, k].rearrange("p e j -> p (e j)"))
+        def XP(u):
+            i, k = divmod(u, K)
+            xtile(u)
+            muk = mu0[:].rearrange("p (e k) -> p e k", k=K)[:, :, k]
+            xk = x_raw[i][:].rearrange("p j (e k) -> p j e k", k=K)[:, :, :, k]
+            for v in range(4):
+                t = pac.tile([P, J, P], F32, name="acc")
+                ps["x", u, v] = t
+                nc.tensor.matmul(t[:], lhsT=nones[:], rhs=muk[:, v * P:(v + 1) * P].unsqueeze(1).to_broadcast([P, J, P]), start=True, stop=False)
+                for j in range(J):
+                    nc.tensor.matmul(t[:, j, :], lhsT=identb[:], rhs=xk[:, j, v * P:(v + 1) * P], start=False, stop=(j == J - 1))
+
+        def XPE(u):
+            for v in range(4):
+                nc.scalar.copy(out=xa[u][:, v * P:(v + 1) * P, :], in_=ps["x", u, v][:].rearrange("p j e -> p e j"))
+
+        def QX(u):
+            i, k = divmod(u, K)
+            nc.vector.quantize_mx(out=xq[:, i, k, :].bitcast(E4M3), scales=xs[:, i, k, :],
+                                  in_=xa[u][:].rearrange("p e j -> p (e j)"))
 
         def Dw(k):
             for c in range(4):
                 a = pac.tile([P, D], F32, name="acc")
                 ps["w", k, c] = a
                 for i in range(G):
-                    nc.tensor.matmul_mx(out=a[:], lhsT=gq[:, i, c, k, :].bitcast(E5M2), lhsT_scale=gs[:, i, c, k, :],
+                    cols = slice(c * P, (c + 1) * P)
+                    nc.tensor.matmul_mx(out=a[:], lhsT=gq[:, i, k, cols].bitcast(E5M2), lhsT_scale=gs[:, i, k, cols],
                                         rhs=xq[:, i, k, :].bitcast(E4M3), rhs_scale=xs[:, i, k, :],
                                         start=(i == 0), stop=(i == G - 1))
 
-        def Fw(k, engs):
-            o_t = stage.tile([P, 4, D], F32, name="o", tag="o", bufs=3)
+        def Fw(k):
+            o_t = stage.tile([P, 4, D], F32, name="ow", tag="o", bufs=3)
             for c in range(4):
-                engs[c](out=o_t[:, c, :], in_=ps["w", k, c][:])
-            nc.sync.dma_start(out=dw[k].rearrange("(c p) e -> p c e", c=4), in_=o_t[:])
-
-        V = nc.vector.tensor_copy
-        S = nc.scalar.copy
+                copier(FE[4 * k + c])(out=o_t[:, c, :], in_=ps["w", k, c][:])
+                if c % 2:
+                    nc.sync.dma_start(out=dw[k, (c - 1) * P:(c + 1) * P, :].rearrange("(c p) e -> p c e", p=P), in_=o_t[:, c - 1:c + 1, :])
 
         with tc.manual_schedule():
-            load_w(0)
-            load_g(0, 0)
-            load_w(1)
-            nc.sync.dma_start(out=mu0[0:1, :], in_=muv)
-            load_x(0, 0)
-            load_w(2)
-            load_w(3)
-            load_g(0, 1)
-            load_g(0, 2)
-            load_g(0, 3)
-            load_x(0, 1)
-            for j in range(J):
-                load_g(1, j)
-            for h in range(2):
-                load_x(1, h)
-
+            for s in L1:
+                load(s)
             T(0)
             mu_spread()
-            wcopy(0, V)
+            wcopy(0)
             C(0)
-            wcopy(1, V)
+            wcopy(1)
             wquant(0)
-            Q(0)
+            wcopy(2)
             wquant(1)
-            wcopy(2, S)
-            wcopy(3, V)
+            wcopy(3)
             wquant(2)
             wquant(3)
-            pend = []
-            for s in range(N):
-                toks = [u for u in range(N) if SLOT[u] == s]
+            un, pend = 0, []
+            for s in range(N + 3):
+                nt = TOKS[s] if s < len(TOKS) else 0
+                toks = list(range(un, un + nt))
+                un += nt
                 if s + 1 < N:
                     T(s + 1)
-                M(s)
+                if s < N:
+                    Q(s)
+                    M(s)
+                for u in toks:
+                    if XE[u] == "P":
+                        XP(u)
                 if s + 1 < N:
                     C(s + 1)
+                for u in pend:
+                    QX(u)
+                    QG(u)
+                pend = toks
                 for u in toks:
-                    X(u)
-                    if u in VA:
+                    if AE[u] == "G":
                         A(u)
-                if s > 0:
+                for k in range(K):
+                    if DS[k] == s:
+                        Dw(k)
+                for u in toks:
+                    if XE[u] == "V":
+                        X(u)
+                if 0 < s <= N and (s - 1) not in IS:
                     I(s - 1)
-                for f in pend:
-                    f()
-                pend = []
-                E(s)
                 for u in toks:
-                    if u not in VA:
+                    if AE[u] == "V":
                         A(u)
-                    pend.append(lambda u=u: QG(u))
-                    if u % 2 == 1:
-                        pend.append(lambda u=u: QX(u // 2))
-                if s + 1 < N:
-                    Q(s + 1)
-                if 3 in [u for u in toks]:
-                    for j in range(J):
-                        load_g(2, j)
-                    for h in range(2):
-                        load_x(2, h)
-                if s >= 9:
-                    Dw(s - 9)
-                    Fw(s - 9, [V, V, V, V])
-            I(N - 1)
-            Dw(3)
-            Fw(3, [S, V, S, V])
+                if s < N:
+                    E(s, [0, 1, 2, 3], "S")
+                for u in toks:
+                    if XE[u] == "P":
+                        XPE(u)
+                for u in toks:
+                    if AE[u] == "S":
+                        A(u)
+                if 0 < s <= N and (s - 1) in IS:
+                    I(s - 1)
+                for k in range(K):
+                    if DS[k] + FL == s:
+                        Fw(k)
+                if s == 4:
+                    for l in L2:
+                        load(l)

@@ -20,15 +20,17 @@ G = B // (P * J)
 DK = D * K
 N = G * J
 
-TOKS = [2,2,0,1,2,0,1,1,2,0,1,0]
-AE = "VVVVVVVVVSVV"
-IS = [0,5]
-FE = "VSVSVVSSVSSVSSSS"
-XE = "VPVPVPVVVVPV"
+XS = [1,2,0,2,1,1,2,0,2,1,0,0]
+AS = [2,2,0,1,1,1,1,0,1,1,1,1]
+AE = "VVVVVVVVSVVV"
+XH = "VPVPVV"
+XI = "SVVVVVSSVVVS"
+IS = [3]
+FE = "SVSSVSVSSSSSSVSV"
 WE = "VVSV"
-DS = [8,9,10,11]
+DS = [10,11,13,13]
 FL = 0
-L1 = ["w0","g00","mu","w1","w2","w3","g01","x00","x01","g02","g03","x10","x11","g10","g11","g12","g13"]
+L1 = ["w0","g00","w1","w2","w3","g01","mu","x00","g02","g03","x01","g10","x10","g11","x11","g12","g13"]
 L2 = ["x20","x21","g20","g21","g22","g23"]
 
 
@@ -37,7 +39,6 @@ def tile_clusternorm1dv3_v_kernel(tc, x, mu, w, g, dx, dw):
     xv = x.rearrange("(g p j) d k -> g p j (d k)", p=P, j=J)
     gv = g.rearrange("(g p j) d k -> g p j (d k)", p=P, j=J)
     dxv = dx.rearrange("(g p j) d k -> g p j (d k)", p=P, j=J)
-    muv = mu.rearrange("(o d) k -> o (d k)", o=1)
 
     with ExitStack() as ctx:
         keep = ctx.enter_context(tc.tile_pool(name="keep", bufs=1))
@@ -50,18 +51,15 @@ def tile_clusternorm1dv3_v_kernel(tc, x, mu, w, g, dx, dw):
         make_identity(nc, ident[:])
         identb = keep.tile([P, P], BF16)
         make_identity(nc, identb[:])
-        gq = keep.tile([P, G, K, D], U32, align_bytes=64)
-        gs = keep.tile([P, G, K, D], U8, align_bytes=64)
+        gq = keep.tile([P, G, 4, K, P], U32, align_bytes=64)
+        gs = keep.tile([P, G, 4, K, P], U8, align_bytes=64)
         xq = keep.tile([P, G, K, D], U32, align_bytes=64)
         xs = keep.tile([P, G, K, D], U8, align_bytes=64)
         wq = keep.tile([P, K, D], U32, align_bytes=64)
         ws = keep.tile([P, K, D], U8, align_bytes=64)
-        mu0 = keep.tile([P, DK], BF16)
-        nc.vector.memset(mu0[:], 0.0)
-        ones = keep.tile([P, P], BF16)
-        nc.gpsimd.memset(ones[:], 1.0)
-        nones = keep.tile([P, P], BF16)
-        nc.gpsimd.memset(nones[:], -1.0)
+        sel = keep.tile([P, P], BF16)
+        nc.gpsimd.memset(sel[:], 0.0)
+        nc.gpsimd.memset(sel[0:1, :], -1.0)
         mub = keep.tile([P, DK], BF16)
 
         g_raw, x_raw, w_raw = {}, {}, {}
@@ -79,7 +77,7 @@ def tile_clusternorm1dv3_v_kernel(tc, x, mu, w, g, dx, dw):
 
         def load(s):
             if s == "mu":
-                nc.sync.dma_start(out=mu0[0:1, :], in_=muv)
+                nc.sync.dma_start(out=mub[:], in_=mu.rearrange("d k -> (d k)").partition_broadcast(P))
                 return
             i = int(s[1])
             if s[0] == "w":
@@ -107,12 +105,6 @@ def tile_clusternorm1dv3_v_kernel(tc, x, mu, w, g, dx, dw):
 
         def wquant(k):
             nc.vector.quantize_mx(out=wq[:, k, :].bitcast(E4M3), scales=ws[:, k, :], in_=wa[k][:].rearrange("p e j -> p (e j)"))
-
-        def mu_spread():
-            for c in range(4):
-                t = pac.tile([P, D], F32, name="acc")
-                nc.tensor.matmul(t[:], lhsT=ones[:], rhs=mu0[:, c * 512:(c + 1) * 512], start=True, stop=True)
-                nc.scalar.copy(out=mub[:, c * 512:(c + 1) * 512], in_=t[:])
 
         def T(n):
             i, j = divmod(n, J)
@@ -157,125 +149,140 @@ def tile_clusternorm1dv3_v_kernel(tc, x, mu, w, g, dx, dw):
             copier("S" if n in IS else "V")(out=o_t[:], in_=m[n][:].rearrange("p k e -> p e k"))
             nc.sync.dma_start(out=dxv[i, :, j, :], in_=o_t[:].rearrange("p e k -> p (e k)"))
 
+        def interleave(e, out, in_):
+            copier(e)(out=out.rearrange("p k (d a) j -> p d k a j", a=2), in_=in_.rearrange("p j (d a k) -> p d k a j", a=2, k=K))
+
         def A(u):
-            i, k = divmod(u, K)
-            t = stage.tile([P, D, J], BF16, align_bytes=64, name="ga", bufs=3)
+            i, c = divmod(u, 4)
+            t = stage.tile([P, K, P, J], BF16, align_bytes=64, name="ga", bufs=3)
             ga[u] = t
-            copier(AE[u])(out=t[:], in_=g_raw[i][:].rearrange("p j (d k) -> p d k j", k=K)[:, :, k, :])
+            interleave(AE[u], t[:], g_raw[i][:, :, c * 512:(c + 1) * 512])
 
         def QG(u):
-            i, k = divmod(u, K)
-            nc.vector.quantize_mx(out=gq[:, i, k, :].bitcast(E5M2), scales=gs[:, i, k, :],
-                                  in_=ga[u][:].rearrange("p d j -> p (d j)"))
+            i, c = divmod(u, 4)
+            nc.vector.quantize_mx(out=gq[:, i, c].rearrange("p k d -> p (k d)").bitcast(E5M2),
+                                  scales=gs[:, i, c].rearrange("p k d -> p (k d)"),
+                                  in_=ga[u][:].rearrange("p k d j -> p (k d j)"))
 
-        def xtile(u):
-            t = stage.tile([P, D, J], BF16, align_bytes=64, name="xa", bufs=3)
-            xa[u] = t
+        def xtile(h):
+            if h not in xa:
+                t = stage.tile([P, K, 2 * P, J], BF16, align_bytes=64, name="xa", bufs=2)
+                xa[h] = t
 
-        def X(u):
-            i, k = divmod(u, K)
-            xtile(u)
-            nc.vector.tensor_sub(out=xa[u][:], in0=x_raw[i][:].rearrange("p j (e k) -> p e k j", k=K)[:, :, k, :],
-                                 in1=mub[:].rearrange("p (e k) -> p e k", k=K)[:, :, k].unsqueeze(2).to_broadcast([P, D, J]))
+        def TN(h):
+            i, b = divmod(h, 2)
+            v = x_raw[i][:, :, b * 1024:(b + 1) * 1024]
+            nc.vector.tensor_sub(out=v, in0=v, in1=mub[:, b * 1024:(b + 1) * 1024].unsqueeze(1).to_broadcast([P, J, 1024]))
 
-        def XP(u):
-            i, k = divmod(u, K)
-            xtile(u)
-            muk = mu0[:].rearrange("p (e k) -> p e k", k=K)[:, :, k]
-            xk = x_raw[i][:].rearrange("p j (e k) -> p j e k", k=K)[:, :, :, k]
-            for v in range(4):
+        def IX(h, z):
+            i, b = divmod(h, 2)
+            xtile(h)
+            lo = (2 * b + z) * 512
+            interleave(XI[2 * h + z], xa[h][:, :, z * P:(z + 1) * P, :], x_raw[i][:, :, lo:lo + 512])
+
+        def XP(h, z):
+            i, b = divmod(h, 2)
+            xtile(h)
+            for v in range(4 * z, 4 * z + 4):
+                lo = b * 1024 + v * P
                 t = pac.tile([P, J, P], F32, name="acc")
-                ps["x", u, v] = t
-                nc.tensor.matmul(t[:], lhsT=nones[:], rhs=muk[:, v * P:(v + 1) * P].unsqueeze(1).to_broadcast([P, J, P]), start=True, stop=False)
+                ps["x", h, v] = t
+                nc.tensor.matmul(t[:], lhsT=sel[:], rhs=mub[:, lo:lo + P].unsqueeze(1).to_broadcast([P, J, P]), start=True, stop=False)
                 for j in range(J):
-                    nc.tensor.matmul(t[:, j, :], lhsT=identb[:], rhs=xk[:, j, v * P:(v + 1) * P], start=False, stop=(j == J - 1))
+                    nc.tensor.matmul(t[:, j, :], lhsT=identb[:], rhs=x_raw[i][:, j, lo:lo + P], start=False, stop=(j == J - 1))
 
-        def XPE(u):
-            for v in range(4):
-                nc.scalar.copy(out=xa[u][:, v * P:(v + 1) * P, :], in_=ps["x", u, v][:].rearrange("p j e -> p e j"))
+        def XPE(h, z):
+            for v in range(4 * z, 4 * z + 4):
+                nc.scalar.copy(out=xa[h][:, :, v * 32:(v + 1) * 32, :], in_=ps["x", h, v][:].rearrange("p j (e k) -> p k e j", k=K))
 
-        def QX(u):
-            i, k = divmod(u, K)
-            nc.vector.quantize_mx(out=xq[:, i, k, :].bitcast(E4M3), scales=xs[:, i, k, :],
-                                  in_=xa[u][:].rearrange("p e j -> p (e j)"))
+        def QX(h):
+            i, b = divmod(h, 2)
+            for k in range(K):
+                nc.vector.quantize_mx(out=xq[:, i, k, b * 256:(b + 1) * 256].bitcast(E4M3), scales=xs[:, i, k, b * 256:(b + 1) * 256],
+                                      in_=xa[h][:, k].rearrange("p e j -> p (e j)"))
 
-        def Dw(k):
-            for c in range(4):
+        def Dw(c):
+            for k in range(K):
                 a = pac.tile([P, D], F32, name="acc")
-                ps["w", k, c] = a
+                ps["w", c, k] = a
                 for i in range(G):
-                    cols = slice(c * P, (c + 1) * P)
-                    nc.tensor.matmul_mx(out=a[:], lhsT=gq[:, i, k, cols].bitcast(E5M2), lhsT_scale=gs[:, i, k, cols],
+                    nc.tensor.matmul_mx(out=a[:], lhsT=gq[:, i, c, k, :].bitcast(E5M2), lhsT_scale=gs[:, i, c, k, :],
                                         rhs=xq[:, i, k, :].bitcast(E4M3), rhs_scale=xs[:, i, k, :],
                                         start=(i == 0), stop=(i == G - 1))
 
-        def Fw(k):
-            o_t = stage.tile([P, 4, D], F32, name="ow", tag="o", bufs=3)
-            for c in range(4):
-                copier(FE[4 * k + c])(out=o_t[:, c, :], in_=ps["w", k, c][:])
-                if c % 2:
-                    nc.sync.dma_start(out=dw[k, (c - 1) * P:(c + 1) * P, :].rearrange("(c p) e -> p c e", p=P), in_=o_t[:, c - 1:c + 1, :])
+        def Fw(c):
+            o_t = stage.tile([P, K, D], F32, name="ow", tag="o", bufs=3)
+            for k in range(K):
+                copier(FE[4 * c + k])(out=o_t[:, k, :], in_=ps["w", c, k][:])
+                if k % 2:
+                    nc.sync.dma_start(out=dw[k - 1:k + 1, c * P:(c + 1) * P, :].rearrange("k p e -> p k e"), in_=o_t[:, k - 1:k + 1, :])
 
         with tc.manual_schedule():
             for s in L1:
                 load(s)
             T(0)
-            mu_spread()
-            wcopy(0)
             C(0)
+            wcopy(0)
             wcopy(1)
             wquant(0)
             wcopy(2)
             wquant(1)
+            Q(0)
             wcopy(3)
             wquant(2)
             wquant(3)
-            un, pend = 0, []
+            an, xn, pend_a, pend_x = 0, 0, [], []
             for s in range(N + 3):
-                nt = TOKS[s] if s < len(TOKS) else 0
-                toks = list(range(un, un + nt))
-                un += nt
+                na, nx = (AS[s], XS[s]) if s < N else (0, 0)
+                at, xt = list(range(an, an + na)), [divmod(p, 2) for p in range(xn, xn + nx)]
+                an += na
+                xn += nx
                 if s + 1 < N:
                     T(s + 1)
-                if s < N:
+                if 0 < s < N:
                     Q(s)
+                if s < N:
                     M(s)
-                for u in toks:
-                    if XE[u] == "P":
-                        XP(u)
+                for h, z in xt:
+                    if XH[h] == "P":
+                        XP(h, z)
                 if s + 1 < N:
                     C(s + 1)
-                for u in pend:
-                    QX(u)
-                    QG(u)
-                pend = toks
-                for u in toks:
-                    if AE[u] == "G":
-                        A(u)
-                for k in range(K):
-                    if DS[k] == s:
-                        Dw(k)
-                for u in toks:
-                    if XE[u] == "V":
-                        X(u)
                 if 0 < s <= N and (s - 1) not in IS:
                     I(s - 1)
-                for u in toks:
+                for h in pend_x:
+                    QX(h)
+                for u in pend_a:
+                    QG(u)
+                for c in range(4):
+                    if DS[c] == s:
+                        Dw(c)
+                for h, z in xt:
+                    if XH[h] == "V" and z == 0:
+                        TN(h)
+                for u in at:
                     if AE[u] == "V":
                         A(u)
+                for h, z in xt:
+                    if XH[h] == "V" and XI[2 * h + z] == "V":
+                        IX(h, z)
                 if s < N:
                     E(s, [0, 1, 2, 3], "S")
-                for u in toks:
-                    if XE[u] == "P":
-                        XPE(u)
-                for u in toks:
+                for h, z in xt:
+                    if XH[h] == "P":
+                        XPE(h, z)
+                    elif XI[2 * h + z] == "S":
+                        IX(h, z)
+                for u in at:
                     if AE[u] == "S":
                         A(u)
                 if 0 < s <= N and (s - 1) in IS:
                     I(s - 1)
-                for k in range(K):
-                    if DS[k] + FL == s:
-                        Fw(k)
+                for c in range(4):
+                    if DS[c] + FL == s:
+                        Fw(c)
+                pend_x = [h for h, z in xt if z == 1]
+                pend_a = at
                 if s == 4:
                     for l in L2:
                         load(l)

@@ -20,17 +20,17 @@ G = B // (P * J)
 DK = D * K
 N = G * J
 
-XS = [1,2,0,2,1,1,2,0,2,1,0,0]
-AS = [2,2,0,1,1,1,1,0,1,1,1,1]
-AE = "VVVVVVVVSVVV"
-XH = "VPVPVV"
-XI = "SVVVVVSSVVVS"
-IS = [3]
-FE = "SVSSVSVSSSSSSVSV"
+XS = [0,1,2,2,0,1,1,2,1,2,0,0]
+AS = [2,1,1,1,0,1,1,1,0,2,1,1]
+AE = "VVVVVVVVVVVV"
+XH = "PVPPVP"
+XI = "VVVVVVVVVVVV"
+IS = []
+FE = "SVSSVSSSVSVSVSSS"
 WE = "VVSV"
 DS = [10,11,13,13]
 FL = 0
-L1 = ["w0","g00","w1","w2","w3","g01","mu","x00","g02","g03","x01","g10","x10","g11","x11","g12","g13"]
+L1 = ["w0","g00","mu","w1","w2","w3","g01","g02","g03","x00","x01","bc","x10","x11","g10","g11","g12","g13"]
 L2 = ["x20","x21","g20","g21","g22","g23"]
 
 
@@ -57,9 +57,9 @@ def tile_clusternorm1dv3_v_kernel(tc, x, mu, w, g, dx, dw):
         xs = keep.tile([P, G, K, D], U8, align_bytes=64)
         wq = keep.tile([P, K, D], U32, align_bytes=64)
         ws = keep.tile([P, K, D], U8, align_bytes=64)
-        sel = keep.tile([P, P], BF16)
-        nc.gpsimd.memset(sel[:], 0.0)
-        nc.gpsimd.memset(sel[0:1, :], -1.0)
+        murow = keep.tile([P, P], BF16)
+        nc.vector.memset(murow[:], 0.0)
+        negmu = keep.tile([P, 16], F32)
         mub = keep.tile([P, DK], BF16)
 
         g_raw, x_raw, w_raw = {}, {}, {}
@@ -77,6 +77,9 @@ def tile_clusternorm1dv3_v_kernel(tc, x, mu, w, g, dx, dw):
 
         def load(s):
             if s == "mu":
+                nc.sync.dma_start(out=murow[0:16, :], in_=mu.rearrange("(b d) k -> b (d k)", b=16))
+                return
+            if s == "bc":
                 nc.sync.dma_start(out=mub[:], in_=mu.rearrange("d k -> (d k)").partition_broadcast(P))
                 return
             i = int(s[1])
@@ -138,15 +141,15 @@ def tile_clusternorm1dv3_v_kernel(tc, x, mu, w, g, dx, dw):
 
         def E(n, ks, e):
             if n not in m:
-                m_t = stage.tile([P, K, D], F32, name="m", bufs=2)
+                m_t = stage.tile([P, D // 4, K, 4], F32, name="m", bufs=2)
                 m[n] = m_t
             for k in ks:
-                copier(e)(out=m[n][:, k, :], in_=ps[n, k][:])
+                copier(e)(out=m[n][:, :, k, :], in_=ps[n, k][:].rearrange("p (q i) -> p q i", i=4))
 
         def I(n):
             i, j = divmod(n, J)
             o_t = stage.tile([P, D, K], F32, name="o", tag="o", bufs=3)
-            copier("S" if n in IS else "V")(out=o_t[:], in_=m[n][:].rearrange("p k e -> p e k"))
+            copier("S" if n in IS else "V")(out=o_t[:].rearrange("p (q i) k -> p q i k", i=4), in_=m[n][:].rearrange("p q k i -> p q i k"))
             nc.sync.dma_start(out=dxv[i, :, j, :], in_=o_t[:].rearrange("p e k -> p (e k)"))
 
         def interleave(e, out, in_):
@@ -180,6 +183,11 @@ def tile_clusternorm1dv3_v_kernel(tc, x, mu, w, g, dx, dw):
             lo = (2 * b + z) * 512
             interleave(XI[2 * h + z], xa[h][:, :, z * P:(z + 1) * P, :], x_raw[i][:, :, lo:lo + 512])
 
+        def mu_columns():
+            t = pac.tile([P, P], BF16, name="acc")
+            nc.tensor.transpose(t[:], murow[:], identb[:])
+            nc.vector.tensor_scalar(out=negmu[:], in0=t[:, 0:16], scalar1=-1.0, scalar2=None, op0=ALU.mult)
+
         def XP(h, z):
             i, b = divmod(h, 2)
             xtile(h)
@@ -187,7 +195,9 @@ def tile_clusternorm1dv3_v_kernel(tc, x, mu, w, g, dx, dw):
                 lo = b * 1024 + v * P
                 t = pac.tile([P, J, P], F32, name="acc")
                 ps["x", h, v] = t
-                nc.tensor.matmul(t[:], lhsT=sel[:], rhs=mub[:, lo:lo + P].unsqueeze(1).to_broadcast([P, J, P]), start=True, stop=False)
+                col = negmu[:, lo // P:lo // P + 1].to_broadcast([P, P])
+                for j in range(J):
+                    nc.tensor.matmul(t[:, j, :], lhsT=col, rhs=ident[:], start=(j == 0), stop=False, is_transpose=True)
                 for j in range(J):
                     nc.tensor.matmul(t[:, j, :], lhsT=identb[:], rhs=x_raw[i][:, j, lo:lo + P], start=False, stop=(j == J - 1))
 
@@ -221,6 +231,7 @@ def tile_clusternorm1dv3_v_kernel(tc, x, mu, w, g, dx, dw):
             for s in L1:
                 load(s)
             T(0)
+            mu_columns()
             C(0)
             wcopy(0)
             wcopy(1)

from contextlib import ExitStack

import concourse.mybir as mybir
from concourse.masks import make_identity

B, D, K = 1536, 512, 4
FLOPS = 2 * 2 * B * D * D * K

F32 = mybir.dt.float32
BF16 = mybir.dt.bfloat16
U32 = mybir.dt.uint32
U8 = mybir.dt.uint8
E4M3 = mybir.dt.float8_e4m3fn_x4
E5M2 = mybir.dt.float8_e5m2_x4
ALU = mybir.AluOpType

P = 128
J = 4
G = B // (P * J)
DK = D * K
N = G * J

XS = [0,1,2,2,0,1,1,2,1,2,0,0]
AS = [2,1,1,1,0,1,1,1,0,2,1,1]
AE = "VVVVVVVVVVVV"
XH = "PVPPVP"
XI = "VVVVVVVVVVVV"
IS = []
FE = "SVSSVSSSVSVSVSSS"
WE = "VVSV"
DS = [10,11,13,13]
FL = 0
L1 = ["w0","g00","mu","w1","w2","w3","g01","g02","g03","x00","x01","bc","x10","x11","g10","g11","g12","g13"]
L2 = ["x20","x21","g20","g21","g22","g23"]


def tile_clusternorm1dv3_v_kernel(tc, x, mu, w, g, dx, dw):
    nc = tc.nc
    xv = x.rearrange("(g p j) d k -> g p j (d k)", p=P, j=J)
    gv = g.rearrange("(g p j) d k -> g p j (d k)", p=P, j=J)
    dxv = dx.rearrange("(g p j) d k -> g p j (d k)", p=P, j=J)

    with ExitStack() as ctx:
        keep = ctx.enter_context(tc.tile_pool(name="keep", bufs=1))
        raw = ctx.enter_context(tc.tile_pool(name="raw", bufs=2))
        stage = ctx.enter_context(tc.tile_pool(name="stage", bufs=2))
        ptr = ctx.enter_context(tc.psum_pool(name="ptr", bufs=2))
        pac = ctx.enter_context(tc.psum_pool(name="pac", bufs=6))

        ident = keep.tile([P, P], F32)
        make_identity(nc, ident[:])
        identb = keep.tile([P, P], BF16)
        make_identity(nc, identb[:])
        gq = keep.tile([P, G, 4, K, P], U32, align_bytes=64)
        gs = keep.tile([P, G, 4, K, P], U8, align_bytes=64)
        xq = keep.tile([P, G, K, D], U32, align_bytes=64)
        xs = keep.tile([P, G, K, D], U8, align_bytes=64)
        wq = keep.tile([P, K, D], U32, align_bytes=64)
        ws = keep.tile([P, K, D], U8, align_bytes=64)
        murow = keep.tile([P, P], BF16)
        nc.vector.memset(murow[:], 0.0)
        negmu = keep.tile([P, 16], F32)
        mub = keep.tile([P, DK], BF16)

        g_raw, x_raw, w_raw = {}, {}, {}
        gd, gdq, gds, ps, m, ga, xa, wa, tr = {}, {}, {}, {}, {}, {}, {}, {}, {}

        def copier(e):
            if e == "V":
                return nc.vector.tensor_copy
            if e == "S":
                return nc.scalar.copy

            def gcopy(out, in_):
                nc.gpsimd.tensor_scalar(out=out, in0=in_, scalar1=1.0, scalar2=0.0, op0=ALU.mult, op1=ALU.add)
            return gcopy

        def load(s):
            if s == "mu":
                nc.sync.dma_start(out=murow[0:16, :], in_=mu.rearrange("(b d) k -> b (d k)", b=16))
                return
            if s == "bc":
                nc.sync.dma_start(out=mub[:], in_=mu.rearrange("d k -> (d k)").partition_broadcast(P))
                return
            i = int(s[1])
            if s[0] == "w":
                if i % 2 == 0:
                    t = stage.tile([P, 2, J, D], BF16, name="wraw", tag="o", bufs=3)
                    w_raw[i // 2] = t
                nc.sync.dma_start(out=w_raw[i // 2][:, i % 2], in_=w[i].rearrange("(p j) e -> p j e", j=J))
            elif s[0] == "g":
                j = int(s[2])
                if i not in g_raw:
                    t = raw.tile([P, J, DK], BF16, name="graw", bufs=2)
                    g_raw[i] = t
                nc.sync.dma_start(out=g_raw[i][:, j, :], in_=gv[i, :, j, :])
            else:
                h = int(s[2])
                if i not in x_raw:
                    t = raw.tile([P, J, DK], BF16, name="xraw", bufs=2)
                    x_raw[i] = t
                nc.sync.dma_start(out=x_raw[i][:, :, h * 1024:(h + 1) * 1024], in_=xv[i, :, :, h * 1024:(h + 1) * 1024])

        def wcopy(k):
            t = stage.tile([P, D, J], BF16, align_bytes=64, name="wa", bufs=2)
            wa[k] = t
            copier(WE[k])(out=t[:], in_=w_raw[k // 2][:, k % 2].rearrange("p j e -> p e j"))

        def wquant(k):
            nc.vector.quantize_mx(out=wq[:, k, :].bitcast(E4M3), scales=ws[:, k, :], in_=wa[k][:].rearrange("p e j -> p (e j)"))

        def T(n):
            i, j = divmod(n, J)
            gw = g_raw[i][:].bitcast(F32)
            for kk in range(2):
                t_ = ptr.tile([P, J, P], F32, name="tr")
                tr[n, kk] = t_
                for t in range(J):
                    nc.tensor.transpose(t_[:, t, :], gw[:, j, 2 * t + kk:1024:8], ident[:])

        def C(n):
            gd_t = stage.tile([P, K, P, J], BF16, align_bytes=64, name="gd", bufs=2)
            gd[n] = gd_t
            for kk in range(2):
                nc.scalar.copy(out=gd_t[:, 2 * kk:2 * kk + 2], in_=tr[n, kk][:].bitcast(BF16).rearrange("q t (m e) -> q e m t", e=2))

        def Q(n):
            q = stage.tile([P, K, P], U32, align_bytes=64, name="gdq")
            s = stage.tile([P, K, P], U8, align_bytes=64, name="gds")
            gdq[n], gds[n] = q, s
            nc.vector.quantize_mx(out=q[:].rearrange("p k m -> p (k m)").bitcast(E5M2),
                                  scales=s[:].rearrange("p k m -> p (k m)"),
                                  in_=gd[n][:].rearrange("p k m t -> p (k m t)"))

        def M(n):
            for k in range(K):
                a = pac.tile([P, D], F32, name="acc")
                ps[n, k] = a
                nc.tensor.matmul_mx(out=a[:], lhsT=gdq[n][:, k, :].bitcast(E5M2), lhsT_scale=gds[n][:, k, :],
                                    rhs=wq[:, k, :].bitcast(E4M3), rhs_scale=ws[:, k, :], start=True, stop=True)

        def E(n, ks, e):
            if n not in m:
                m_t = stage.tile([P, D // 4, K, 4], F32, name="m", bufs=2)
                m[n] = m_t
            for k in ks:
                copier(e)(out=m[n][:, :, k, :], in_=ps[n, k][:].rearrange("p (q i) -> p q i", i=4))

        def I(n):
            i, j = divmod(n, J)
            o_t = stage.tile([P, D, K], F32, name="o", tag="o", bufs=3)
            copier("S" if n in IS else "V")(out=o_t[:].rearrange("p (q i) k -> p q i k", i=4), in_=m[n][:].rearrange("p q k i -> p q i k"))
            nc.sync.dma_start(out=dxv[i, :, j, :], in_=o_t[:].rearrange("p e k -> p (e k)"))

        def interleave(e, out, in_):
            copier(e)(out=out.rearrange("p k (d a) j -> p d k a j", a=2), in_=in_.rearrange("p j (d a k) -> p d k a j", a=2, k=K))

        def A(u):
            i, c = divmod(u, 4)
            t = stage.tile([P, K, P, J], BF16, align_bytes=64, name="ga", bufs=3)
            ga[u] = t
            interleave(AE[u], t[:], g_raw[i][:, :, c * 512:(c + 1) * 512])

        def QG(u):
            i, c = divmod(u, 4)
            nc.vector.quantize_mx(out=gq[:, i, c].rearrange("p k d -> p (k d)").bitcast(E5M2),
                                  scales=gs[:, i, c].rearrange("p k d -> p (k d)"),
                                  in_=ga[u][:].rearrange("p k d j -> p (k d j)"))

        def xtile(h):
            if h not in xa:
                t = stage.tile([P, K, 2 * P, J], BF16, align_bytes=64, name="xa", bufs=2)
                xa[h] = t

        def TN(h):
            i, b = divmod(h, 2)
            v = x_raw[i][:, :, b * 1024:(b + 1) * 1024]
            nc.vector.tensor_sub(out=v, in0=v, in1=mub[:, b * 1024:(b + 1) * 1024].unsqueeze(1).to_broadcast([P, J, 1024]))

        def IX(h, z):
            i, b = divmod(h, 2)
            xtile(h)
            lo = (2 * b + z) * 512
            interleave(XI[2 * h + z], xa[h][:, :, z * P:(z + 1) * P, :], x_raw[i][:, :, lo:lo + 512])

        def mu_columns():
            t = pac.tile([P, P], BF16, name="acc")
            nc.tensor.transpose(t[:], murow[:], identb[:])
            nc.vector.tensor_scalar(out=negmu[:], in0=t[:, 0:16], scalar1=-1.0, scalar2=None, op0=ALU.mult)

        def XP(h, z):
            i, b = divmod(h, 2)
            xtile(h)
            for v in range(4 * z, 4 * z + 4):
                lo = b * 1024 + v * P
                t = pac.tile([P, J, P], F32, name="acc")
                ps["x", h, v] = t
                col = negmu[:, lo // P:lo // P + 1].to_broadcast([P, P])
                for j in range(J):
                    nc.tensor.matmul(t[:, j, :], lhsT=col, rhs=ident[:], start=(j == 0), stop=False, is_transpose=True)
                for j in range(J):
                    nc.tensor.matmul(t[:, j, :], lhsT=identb[:], rhs=x_raw[i][:, j, lo:lo + P], start=False, stop=(j == J - 1))

        def XPE(h, z):
            for v in range(4 * z, 4 * z + 4):
                nc.scalar.copy(out=xa[h][:, :, v * 32:(v + 1) * 32, :], in_=ps["x", h, v][:].rearrange("p j (e k) -> p k e j", k=K))

        def QX(h):
            i, b = divmod(h, 2)
            for k in range(K):
                nc.vector.quantize_mx(out=xq[:, i, k, b * 256:(b + 1) * 256].bitcast(E4M3), scales=xs[:, i, k, b * 256:(b + 1) * 256],
                                      in_=xa[h][:, k].rearrange("p e j -> p (e j)"))

        def Dw(c):
            for k in range(K):
                a = pac.tile([P, D], F32, name="acc")
                ps["w", c, k] = a
                for i in range(G):
                    nc.tensor.matmul_mx(out=a[:], lhsT=gq[:, i, c, k, :].bitcast(E5M2), lhsT_scale=gs[:, i, c, k, :],
                                        rhs=xq[:, i, k, :].bitcast(E4M3), rhs_scale=xs[:, i, k, :],
                                        start=(i == 0), stop=(i == G - 1))

        def Fw(c):
            o_t = stage.tile([P, K, D], F32, name="ow", tag="o", bufs=3)
            for k in range(K):
                copier(FE[4 * c + k])(out=o_t[:, k, :], in_=ps["w", c, k][:])
                if k % 2:
                    nc.sync.dma_start(out=dw[k - 1:k + 1, c * P:(c + 1) * P, :].rearrange("k p e -> p k e"), in_=o_t[:, k - 1:k + 1, :])

        with tc.manual_schedule():
            for s in L1:
                load(s)
            T(0)
            mu_columns()
            C(0)
            wcopy(0)
            wcopy(1)
            wquant(0)
            wcopy(2)
            wquant(1)
            Q(0)
            wcopy(3)
            wquant(2)
            wquant(3)
            an, xn, pend_a, pend_x = 0, 0, [], []
            for s in range(N + 3):
                na, nx = (AS[s], XS[s]) if s < N else (0, 0)
                at, xt = list(range(an, an + na)), [divmod(p, 2) for p in range(xn, xn + nx)]
                an += na
                xn += nx
                if s + 1 < N:
                    T(s + 1)
                if 0 < s < N:
                    Q(s)
                if s < N:
                    M(s)
                for h, z in xt:
                    if XH[h] == "P":
                        XP(h, z)
                if s + 1 < N:
                    C(s + 1)
                if 0 < s <= N and (s - 1) not in IS:
                    I(s - 1)
                for h in pend_x:
                    QX(h)
                for u in pend_a:
                    QG(u)
                for c in range(4):
                    if DS[c] == s:
                        Dw(c)
                for h, z in xt:
                    if XH[h] == "V" and z == 0:
                        TN(h)
                for u in at:
                    if AE[u] == "V":
                        A(u)
                for h, z in xt:
                    if XH[h] == "V" and XI[2 * h + z] == "V":
                        IX(h, z)
                if s < N:
                    E(s, [0, 1, 2, 3], "S")
                for h, z in xt:
                    if XH[h] == "P":
                        XPE(h, z)
                    elif XI[2 * h + z] == "S":
                        IX(h, z)
                for u in at:
                    if AE[u] == "S":
                        A(u)
                if 0 < s <= N and (s - 1) in IS:
                    I(s - 1)
                for c in range(4):
                    if DS[c] + FL == s:
                        Fw(c)
                pend_x = [h for h, z in xt if z == 1]
                pend_a = at
                if s == 4:
                    for l in L2:
                        load(l)
